import numpy as np
import ml_dtypes


def mxq(x, axis, fmt="e4m3"):
    dtype, down = {"e4m3": (ml_dtypes.float8_e4m3fn, 7), "e5m2": (ml_dtypes.float8_e5m2, 14)}[fmt]
    v = np.moveaxis(np.asarray(x, np.float32).astype(ml_dtypes.bfloat16).astype(np.float64), axis, -1)
    blocks = v.reshape(v.shape[:-1] + (-1, 32))
    amax = np.abs(blocks).max(-1, keepdims=True)
    byte = np.maximum(np.where(amax > 0, np.frexp(amax)[1] - 1 + 127, 0) - down, 1)
    scale = np.exp2(byte - 127.0)
    codes = (blocks / scale).astype(np.float32).astype(dtype).astype(np.float64)
    return np.moveaxis((codes * scale).reshape(v.shape), -1, axis)


WIDE = False


def mx_kscale(k):
    if not WIDE:
        return np.ones(k)
    levels = np.array([10, -10, 5, -5, 0])
    if k % 512:
        return np.exp2(np.random.permutation(np.resize(levels, k // 32))).repeat(32)
    a = np.empty((k // 512, 16))
    for p in range(k // 512):
        a[p, :8] = np.random.permutation(np.resize(levels, 8))
        for g in range(8):
            far = levels[np.abs(levels - a[p, g]) >= 10]
            a[p, g + 8] = far[np.random.randint(len(far))]
    return np.exp2(a.ravel()).repeat(32)


BF16 = ml_dtypes.bfloat16


def bf(x):
    return np.asarray(x, np.float32).astype(BF16)


def f64(x):
    return np.asarray(x).astype(np.float64)


LMAX, MMAX, C_IN, C_OUT, E, D_EMB = 6, 2, 512, 128, 256, 8
M_SIZE = [LMAX + 1] + [LMAX - m + 1 for m in range(1, MMAX + 1)]
NUM_COEFFS = M_SIZE[0] + 2 * sum(M_SIZE[1:])
K0, K1, K2 = M_SIZE[0] * C_IN, M_SIZE[1] * C_IN, M_SIZE[2] * C_IN


def setup_inputs():
    s0, s1, s2 = mx_kscale(K0), mx_kscale(K1), mx_kscale(K2)
    s = np.concatenate([s0.reshape(-1, C_IN), s1.reshape(-1, C_IN), s1.reshape(-1, C_IN), s2.reshape(-1, C_IN), s2.reshape(-1, C_IN)], axis=0)
    return {"edge_feats": bf(np.random.standard_normal((E, NUM_COEFFS, C_IN)) * s[None, :, :]),
            "edge_embeds": bf(np.random.standard_normal((E, D_EMB))),
            "W0": bf(np.random.standard_normal((K0, M_SIZE[0] * C_OUT)) / np.sqrt(K0) / s0[:, None]),
            "b0": bf(np.random.standard_normal(M_SIZE[0] * C_OUT) * 0.3),
            "W1": bf(np.random.standard_normal((K1, 2 * M_SIZE[1] * C_OUT)) / np.sqrt(K1) / s1[:, None]),
            "W2": bf(np.random.standard_normal((K2, 2 * M_SIZE[2] * C_OUT)) / np.sqrt(K2) / s2[:, None])}


def reference(edge_feats, edge_embeds, W0, b0, W1, W2):
    edge_feats = f64(edge_feats)
    num_edges = f64(edge_embeds).shape[0]
    feats_0 = edge_feats[:, :M_SIZE[0]].reshape(num_edges, -1)
    feats_0 = (mxq(feats_0, 1, "e4m3") @ mxq(f64(W0), 0, "e4m3")) + f64(b0)
    feats_out = [feats_0.reshape(num_edges, -1, C_OUT)]
    offset = M_SIZE[0]
    Wm_list = [f64(W1), f64(W2)]
    for m in range(1, MMAX + 1):
        feats_m = edge_feats[:, offset:offset + 2 * M_SIZE[m]].reshape(num_edges, 2, -1)
        offset += 2 * M_SIZE[m]
        feats_m = mxq(feats_m, 2, "e4m3") @ mxq(Wm_list[m - 1], 0, "e4m3")
        feats_r, feats_i = np.split(feats_m, 2, axis=2)
        feats_m_r = feats_r[:, 0] - feats_i[:, 1]
        feats_m_i = feats_r[:, 1] + feats_i[:, 0]
        feats_out.append(feats_m_r.reshape(num_edges, -1, C_OUT))
        feats_out.append(feats_m_i.reshape(num_edges, -1, C_OUT))
    return np.concatenate(feats_out, axis=1)

@@ -1,0 +1,226 @@
+from contextlib import ExitStack
+
+import concourse.mybir as mybir
+from concourse.masks import make_identity
+
+F32 = mybir.dt.float32
+BF16 = mybir.dt.bfloat16
+U32 = mybir.dt.uint32
+U8 = mybir.dt.uint8
+FP8X4 = mybir.dt.float8_e4m3fn_x4
+
+P = 128
+PACK = 4
+K_PASS = P * PACK
+C_OUT = 128
+EDGE_TILES = 2
+BANK = 512
+LOAD_COEFFS = 4
+RAW_PASSES = 4
+
+FLOPS = 2 * 256 * (3584 * 896 + 2 * 3072 * 1536 + 2 * 2560 * 1280)
+
+
+def power_of_two_pieces(width, largest):
+    pieces = []
+    start = 0
+    size = largest
+    while start < width:
+        while size > width - start:
+            size = size // 2
+        pieces.append((start, size))
+        start += size
+    return pieces
+
+
+def tile_so2convolution_kernel(tc, edge_feats, edge_embeds, W0, b0, W1, W2, out):
+    nc = tc.nc
+    orders = [(W1, 7, 6, True), (W2, 19, 5, True), (W0, 0, 7, False)]
+    passes = []
+    imaginary = []
+    for m, (weight, first, count, is_complex) in enumerate(orders):
+        passes.extend([(m, g) for g in range(count)])
+        if is_complex:
+            imaginary.extend(range(first + count, first + 2 * count))
+
+    with ExitStack() as ctx:
+        ctx.enter_context(tc.manual_schedule())
+        const = ctx.enter_context(tc.tile_pool(name="const", bufs=1))
+        feats = ctx.enter_context(tc.tile_pool(name="feats", bufs=1))
+        xload = ctx.enter_context(tc.tile_pool(name="xload", bufs=3))
+        xwork = ctx.enter_context(tc.tile_pool(name="xwork", bufs=4))
+        wload = ctx.enter_context(tc.tile_pool(name="wload", bufs=RAW_PASSES))
+        wwork = ctx.enter_context(tc.tile_pool(name="wwork", bufs=3))
+        wquant = ctx.enter_context(tc.tile_pool(name="wquant", bufs=3))
+        result = ctx.enter_context(tc.tile_pool(name="result", bufs=8))
+        psum = ctx.enter_context(tc.psum_pool(name="psum", bufs=8))
+
+        identity = const.tile([P, P], F32)
+        make_identity(nc, identity[:])
+
+        ones = const.tile([P, P], BF16)
+        nc.vector.memset(ones[:], 1.0)
+        bias_row = const.tile([P, 2 * BANK], BF16)
+        nc.vector.memset(bias_row[:], 0.0)
+        nc.scalar.dma_start(out=bias_row[0:1, 0 : 7 * C_OUT], in_=b0.rearrange("(o n) -> o n", o=1))
+
+        x_codes = {}
+        x_scales = {}
+        neg_codes = {}
+        neg_scales = {}
+        loads = []
+        load_size = 1
+        for first, last in [(7, 29), (0, 7)]:
+            c0 = first
+            while c0 < last:
+                n_coeffs = min(load_size, last - c0)
+                loads.append((c0, n_coeffs))
+                c0 += n_coeffs
+                load_size = min(2 * load_size, LOAD_COEFFS)
+        for c0, n_coeffs in loads:
+            xraw = xload.tile([P, EDGE_TILES * n_coeffs * K_PASS], BF16)
+            nc.sync.dma_start(
+                out=xraw[:].rearrange("p (t x) -> p t x", t=EDGE_TILES),
+                in_=edge_feats[:, c0 : c0 + n_coeffs, :].rearrange("(t p) c k -> p t (c k)", p=P),
+            )
+            xwords = xraw[:].bitcast(F32)
+            for j in range(n_coeffs):
+                c = c0 + j
+                bank = psum.tile([P, BANK], F32, tag="bank")
+                for t in range(EDGE_TILES):
+                    for u in range(2):
+                        w0 = (t * n_coeffs + j) * 2 * P
+                        s = 2 * t + u
+                        nc.tensor.transpose(bank[:, s * P : (s + 1) * P], xwords[:, w0 + u : w0 + 2 * P : 2], identity[:])
+                xg = xwork.tile([P, EDGE_TILES * P * PACK], BF16, align_bytes=64)
+                nc.scalar.copy(
+                    out=xg[:].bitcast(F32).rearrange("p (t e u) -> p t e u", t=EDGE_TILES, u=2),
+                    in_=bank[:].rearrange("p (t u e) -> p t e u", t=EDGE_TILES, u=2),
+                )
+                if c in imaginary:
+                    xn = xwork.tile([P, EDGE_TILES * P * PACK], BF16, align_bytes=64)
+                    nc.vector.tensor_scalar_mul(out=xn[:], in0=xg[:], scalar1=-1.0)
+                x_codes[c] = feats.tile([P, EDGE_TILES * P], U32, name="xq%d" % c, align_bytes=64)
+                x_scales[c] = feats.tile([P, EDGE_TILES * P], U8, name="xs%d" % c, align_bytes=64)
+                nc.vector.quantize_mx(out=x_codes[c][:].bitcast(FP8X4), scales=x_scales[c][:], in_=xg[:])
+                if c in imaginary:
+                    neg_codes[c] = feats.tile([P, EDGE_TILES * P], U32, name="nq%d" % c, align_bytes=64)
+                    neg_scales[c] = feats.tile([P, EDGE_TILES * P], U8, name="ns%d" % c, align_bytes=64)
+                    nc.vector.quantize_mx(out=neg_codes[c][:].bitcast(FP8X4), scales=neg_scales[c][:], in_=xn[:])
+
+        bias = const.tile([P, 2 * BANK], F32)
+        for a in range(0, 2 * BANK, BANK):
+            spread = psum.tile([P, BANK], F32, tag="bank")
+            nc.tensor.matmul(spread[:], lhsT=ones[:], rhs=bias_row[:, a : a + BANK], start=True, stop=True)
+            nc.vector.tensor_copy(out=bias[:, a : a + BANK], in_=spread[:])
+
+        raw = {}
+        grouped = {}
+        w_codes = {}
+        w_scales = {}
+        acc = {}
+        stores = []
+
+        def load(i):
+            m, g = passes[i]
+            weight = orders[m][0]
+            raw[i] = wload.tile([P, PACK, weight.shape[1]], BF16, name="wraw%d" % i, tag="wraw")
+            nc.sync.dma_start(
+                out=raw[i][:],
+                in_=weight[g * K_PASS : (g + 1) * K_PASS, :].rearrange("(p j) n -> p j n", j=PACK),
+            )
+
+        def regroup(i):
+            n_cols = orders[passes[i][0]][0].shape[1]
+            half = n_cols // 2
+            grouped[i] = wwork.tile([P, n_cols, PACK], BF16, name="wg%d" % i, tag="wg", align_bytes=64)
+            nc.vector.tensor_copy(
+                out=grouped[i][:, 0:half, :].rearrange("p (c i) t -> p c t i", i=4),
+                in_=raw[i][:, :, 0:half].rearrange("p t (c i) -> p c t i", i=4),
+            )
+            nc.scalar.copy(
+                out=grouped[i][:, half:n_cols, :].rearrange("p (c i) t -> p c t i", i=4),
+                in_=raw[i][:, :, half:n_cols].rearrange("p t (c i) -> p c t i", i=4),
+            )
+
+        def quantise(i):
+            n_cols = orders[passes[i][0]][0].shape[1]
+            w_codes[i] = wquant.tile([P, n_cols], U32, name="wq%d" % i, tag="wq", align_bytes=64)
+            w_scales[i] = wquant.tile([P, n_cols], U8, name="ws%d" % i, tag="ws", align_bytes=64)
+            for a, w in power_of_two_pieces(n_cols, 1024):
+                nc.vector.quantize_mx(
+                    out=w_codes[i][:, a : a + w].bitcast(FP8X4),
+                    scales=w_scales[i][:, a : a + w],
+                    in_=grouped[i][:, a : a + w, :].rearrange("p w j -> p (w j)"),
+                )
+
+        def multiply(i):
+            m, g = passes[i]
+            weight, first, count, is_complex = orders[m]
+            width = count * C_OUT
+            re = first + g
+            im = first + count + g
+            for t in range(EDGE_TILES):
+                edges = slice(t * P, (t + 1) * P)
+                for part in range(2 if is_complex else 1):
+                    if not is_complex:
+                        terms = [(x_codes[re], x_scales[re], 0)]
+                    elif part == 0:
+                        terms = [(x_codes[re], x_scales[re], 0), (neg_codes[im], neg_scales[im], width)]
+                    else:
+                        terms = [(x_codes[im], x_scales[im], 0), (x_codes[re], x_scales[re], width)]
+                    for a, w in power_of_two_pieces(width, BANK):
+                        if g == 0:
+                            acc[(m, t, part, a)] = psum.tile([P, BANK], F32, tag="bank", name="acc_%d_%d_%d_%d" % (m, t, part, a))
+                        for k, (codes, scales, offset) in enumerate(terms):
+                            cols = slice(offset + a, offset + a + w)
+                            nc.tensor.matmul_mx(
+                                out=acc[(m, t, part, a)][:, 0:w],
+                                lhsT=codes[:, edges].bitcast(FP8X4),
+                                lhsT_scale=scales[:, edges],
+                                rhs=w_codes[i][:, cols].bitcast(FP8X4),
+                                rhs_scale=w_scales[i][:, cols],
+                                start=(g == 0 and k == 0),
+                                stop=(g == count - 1 and k == len(terms) - 1),
+                            )
+
+        def finish(m):
+            weight, first, count, is_complex = orders[m]
+            width = count * C_OUT
+            for t in range(EDGE_TILES):
+                for part in range(2 if is_complex else 1):
+                    stage = result.tile([P, width], F32)
+                    for a, w in power_of_two_pieces(width, BANK):
+                        if not is_complex:
+                            nc.vector.tensor_tensor(
+                                out=stage[:, a : a + w],
+                                in0=acc[(m, t, part, a)][:, 0:w],
+                                in1=bias[:, a : a + w],
+                                op=mybir.AluOpType.add,
+                            )
+                        elif part == 0:
+                            nc.scalar.copy(out=stage[:, a : a + w], in_=acc[(m, t, part, a)][:, 0:w])
+                        else:
+                            nc.vector.tensor_copy(out=stage[:, a : a + w], in_=acc[(m, t, part, a)][:, 0:w])
+                    c0 = first + part * count
+                    stores.append((out[t * P : (t + 1) * P, c0 : c0 + count, :].rearrange("p c d -> p (c d)"), stage))
+
+        for i in range(RAW_PASSES):
+            load(i)
+        for s in range(len(passes) + 2):
+            if s < len(passes):
+                regroup(s)
+            if s + RAW_PASSES < len(passes):
+                load(s + RAW_PASSES)
+            if 1 <= s <= len(passes):
+                quantise(s - 1)
+            if s >= 2:
+                m, g = passes[s - 2]
+                if g == orders[m][2] - 1:
+                    finish(m)
+            if 1 <= s <= len(passes):
+                multiply(s - 1)
+            if s + RAW_PASSES >= len(passes) - 1:
+                for target, stage in stores:
+                    nc.sync.dma_start(out=target, in_=stage[:])
+                stores = []

@@ -135,12 +135,12 @@ def tile_so2convolution_kernel(tc, edge_feats, edge_embeds, W0, b0, W1, W2, out)
             half = n_cols // 2
             grouped[i] = wwork.tile([P, n_cols, PACK], BF16, name="wg%d" % i, tag="wg", align_bytes=64)
             nc.vector.tensor_copy(
-                out=grouped[i][:, 0:half, :].rearrange("p (c i) t -> p c t i", i=4),
-                in_=raw[i][:, :, 0:half].rearrange("p t (c i) -> p c t i", i=4),
+                out=grouped[i][:, 0:half, :].rearrange("p (c i) t -> p c t i", i=8),
+                in_=raw[i][:, :, 0:half].rearrange("p t (c i) -> p c t i", i=8),
             )
             nc.scalar.copy(
-                out=grouped[i][:, half:n_cols, :].rearrange("p (c i) t -> p c t i", i=4),
-                in_=raw[i][:, :, half:n_cols].rearrange("p t (c i) -> p c t i", i=4),
+                out=grouped[i][:, half:n_cols, :].rearrange("p (c i) t -> p c t i", i=8),
+                in_=raw[i][:, :, half:n_cols].rearrange("p t (c i) -> p c t i", i=8),
             )
 
         def quantise(i):

@@ -108,11 +108,11 @@ def tile_so2convolution_kernel(tc, edge_feats, edge_embeds, W0, b0, W1, W2, out)
                     neg_scales[c] = feats.tile([P, EDGE_TILES * P], U8, name="ns%d" % c, align_bytes=64)
                     nc.vector.quantize_mx(out=neg_codes[c][:].bitcast(FP8X4), scales=neg_scales[c][:], in_=xn[:])
 
-        bias = const.tile([P, 2 * BANK], F32)
-        for a in range(0, 2 * BANK, BANK):
-            spread = psum.tile([P, BANK], F32, tag="bank")
-            nc.tensor.matmul(spread[:], lhsT=ones[:], rhs=bias_row[:, a : a + BANK], start=True, stop=True)
-            nc.vector.tensor_copy(out=bias[:, a : a + BANK], in_=spread[:])
+        bias = const.tile([P, 7 * C_OUT], BF16)
+        spread = psum.tile([P, 2 * BANK], BF16, tag="bank")
+        for a, b in [(0, BANK), (BANK, 7 * C_OUT)]:
+            nc.tensor.matmul(spread[:, a:b], lhsT=ones[:], rhs=bias_row[:, a:b], start=True, stop=True)
+        nc.vector.tensor_copy(out=bias[:], in_=spread[:, 0 : 7 * C_OUT])
 
         raw = {}
         grouped = {}
@@ -198,10 +198,8 @@ def tile_so2convolution_kernel(tc, edge_feats, edge_embeds, W0, b0, W1, W2, out)
                                 in1=bias[:, a : a + w],
                                 op=mybir.AluOpType.add,
                             )
-                        elif part == 0:
-                            nc.scalar.copy(out=stage[:, a : a + w], in_=acc[(m, t, part, a)][:, 0:w])
                         else:
-                            nc.vector.tensor_copy(out=stage[:, a : a + w], in_=acc[(m, t, part, a)][:, 0:w])
+                            nc.scalar.copy(out=stage[:, a : a + w], in_=acc[(m, t, part, a)][:, 0:w])
                     c0 = first + part * count
                     stores.append((out[t * P : (t + 1) * P, c0 : c0 + count, :].rearrange("p c d -> p (c d)"), stage))
 

@@ -16,6 +16,11 @@ C_OUT = 128
 EDGE_TILES = 2
 BANK = 512
 LOAD_COEFFS = 4
+SCALAR_MORE = 16
+SCALAR_LESS = 96
+HEAD_CUT = 640
+LAST_A = 384
+LAST_B = 768
 RAW_PASSES = 4
 
 FLOPS = 2 * 256 * (3584 * 896 + 2 * 3072 * 1536 + 2 * 2560 * 1280)
@@ -48,7 +53,7 @@ def tile_so2convolution_kernel(tc, edge_feats, edge_embeds, W0, b0, W1, W2, out)
         const = ctx.enter_context(tc.tile_pool(name="const", bufs=1))
         feats = ctx.enter_context(tc.tile_pool(name="feats", bufs=1))
         xload = ctx.enter_context(tc.tile_pool(name="xload", bufs=3))
-        xwork = ctx.enter_context(tc.tile_pool(name="xwork", bufs=4))
+        xwork = ctx.enter_context(tc.tile_pool(name="xwork", bufs=5))
         wload = ctx.enter_context(tc.tile_pool(name="wload", bufs=RAW_PASSES))
         wwork = ctx.enter_context(tc.tile_pool(name="wwork", bufs=3))
         wquant = ctx.enter_context(tc.tile_pool(name="wquant", bufs=3))
@@ -64,19 +69,59 @@ def tile_so2convolution_kernel(tc, edge_feats, edge_embeds, W0, b0, W1, W2, out)
         nc.vector.memset(bias_row[:], 0.0)
         nc.scalar.dma_start(out=bias_row[0:1, 0 : 7 * C_OUT], in_=b0.rearrange("(o n) -> o n", o=1))
 
+        raw = {}
+        grouped = {}
+        w_codes = {}
+        w_scales = {}
+        acc = {}
+        stores = []
+
+        def load(i, cuts):
+            m, g = passes[i]
+            weight = orders[m][0]
+            raw[i] = wload.tile([P, PACK, weight.shape[1]], BF16, name="wraw%d" % i, tag="wraw")
+            rows = weight[g * K_PASS : (g + 1) * K_PASS, :].rearrange("(p j) n -> p j n", j=PACK)
+            for a, b in cuts or [(0, weight.shape[1])]:
+                nc.sync.dma_start(out=raw[i][:, :, a:b], in_=rows[:, :, a:b])
+
+        def regroup(i, engine_copy, a, b):
+            if i not in grouped:
+                n_cols = orders[passes[i][0]][0].shape[1]
+                grouped[i] = wwork.tile([P, n_cols, PACK], BF16, name="wg%d" % i, tag="wg", align_bytes=64)
+            engine_copy(
+                out=grouped[i][:, a:b, :].rearrange("p (c i) t -> p c t i", i=8),
+                in_=raw[i][:, :, a:b].rearrange("p t (c i) -> p c t i", i=8),
+            )
+
+        def quantise(i, parts):
+            n_cols = orders[passes[i][0]][0].shape[1]
+            if i not in w_codes:
+                w_codes[i] = wquant.tile([P, n_cols], U32, name="wq%d" % i, tag="wq", align_bytes=64)
+                w_scales[i] = wquant.tile([P, n_cols], U8, name="ws%d" % i, tag="ws", align_bytes=64)
+            for a, w in parts:
+                nc.vector.quantize_mx(
+                    out=w_codes[i][:, a : a + w].bitcast(FP8X4),
+                    scales=w_scales[i][:, a : a + w],
+                    in_=grouped[i][:, a : a + w, :].rearrange("p w j -> p (w j)"),
+                )
+
+        load(0, [(2 * BANK, 3 * BANK), (0, HEAD_CUT), (HEAD_CUT, 2 * BANK)])
+        regroup(0, nc.vector.tensor_copy, 2 * BANK, 3 * BANK)
+        regroup(0, nc.scalar.copy, 0, HEAD_CUT)
+        regroup(0, nc.vector.tensor_copy, HEAD_CUT, 2 * BANK)
+        quantise(0, [(2 * BANK, BANK), (0, 2 * BANK)])
+
         x_codes = {}
         x_scales = {}
         neg_codes = {}
         neg_scales = {}
         loads = []
-        load_size = 1
         for first, last in [(7, 29), (0, 7)]:
             c0 = first
             while c0 < last:
-                n_coeffs = min(load_size, last - c0)
+                n_coeffs = min(LOAD_COEFFS if loads else LOAD_COEFFS // 2, last - c0)
                 loads.append((c0, n_coeffs))
                 c0 += n_coeffs
-                load_size = min(2 * load_size, LOAD_COEFFS)
         for c0, n_coeffs in loads:
             xraw = xload.tile([P, EDGE_TILES * n_coeffs * K_PASS], BF16)
             nc.sync.dma_start(
@@ -114,47 +159,7 @@ def tile_so2convolution_kernel(tc, edge_feats, edge_embeds, W0, b0, W1, W2, out)
             nc.tensor.matmul(spread[:, a:b], lhsT=ones[:], rhs=bias_row[:, a:b], start=True, stop=True)
         nc.vector.tensor_copy(out=bias[:], in_=spread[:, 0 : 7 * C_OUT])
 
-        raw = {}
-        grouped = {}
-        w_codes = {}
-        w_scales = {}
-        acc = {}
-        stores = []
-
-        def load(i):
-            m, g = passes[i]
-            weight = orders[m][0]
-            raw[i] = wload.tile([P, PACK, weight.shape[1]], BF16, name="wraw%d" % i, tag="wraw")
-            nc.sync.dma_start(
-                out=raw[i][:],
-                in_=weight[g * K_PASS : (g + 1) * K_PASS, :].rearrange("(p j) n -> p j n", j=PACK),
-            )
-
-        def regroup(i):
-            n_cols = orders[passes[i][0]][0].shape[1]
-            half = n_cols // 2
-            grouped[i] = wwork.tile([P, n_cols, PACK], BF16, name="wg%d" % i, tag="wg", align_bytes=64)
-            nc.vector.tensor_copy(
-                out=grouped[i][:, 0:half, :].rearrange("p (c i) t -> p c t i", i=8),
-                in_=raw[i][:, :, 0:half].rearrange("p t (c i) -> p c t i", i=8),
-            )
-            nc.scalar.copy(
-                out=grouped[i][:, half:n_cols, :].rearrange("p (c i) t -> p c t i", i=8),
-                in_=raw[i][:, :, half:n_cols].rearrange("p t (c i) -> p c t i", i=8),
-            )
-
-        def quantise(i):
-            n_cols = orders[passes[i][0]][0].shape[1]
-            w_codes[i] = wquant.tile([P, n_cols], U32, name="wq%d" % i, tag="wq", align_bytes=64)
-            w_scales[i] = wquant.tile([P, n_cols], U8, name="ws%d" % i, tag="ws", align_bytes=64)
-            for a, w in power_of_two_pieces(n_cols, 1024):
-                nc.vector.quantize_mx(
-                    out=w_codes[i][:, a : a + w].bitcast(FP8X4),
-                    scales=w_scales[i][:, a : a + w],
-                    in_=grouped[i][:, a : a + w, :].rearrange("p w j -> p (w j)"),
-                )
-
-        def multiply(i):
+        def multiply(i, chosen=None):
             m, g = passes[i]
             weight, first, count, is_complex = orders[m]
             width = count * C_OUT
@@ -169,7 +174,7 @@ def tile_so2convolution_kernel(tc, edge_feats, edge_embeds, W0, b0, W1, W2, out)
                         terms = [(x_codes[re], x_scales[re], 0), (neg_codes[im], neg_scales[im], width)]
                     else:
                         terms = [(x_codes[im], x_scales[im], 0), (x_codes[re], x_scales[re], width)]
-                    for a, w in power_of_two_pieces(width, BANK):
+                    for a, w in chosen or power_of_two_pieces(width, BANK):
                         if g == 0:
                             acc[(m, t, part, a)] = psum.tile([P, BANK], F32, tag="bank", name="acc_%d_%d_%d_%d" % (m, t, part, a))
                         for k, (codes, scales, offset) in enumerate(terms):
@@ -184,41 +189,69 @@ def tile_so2convolution_kernel(tc, edge_feats, edge_embeds, W0, b0, W1, W2, out)
                                 stop=(g == count - 1 and k == len(terms) - 1),
                             )
 
+        def rows_of_out(m, t, part, a, w):
+            weight, first, count, is_complex = orders[m]
+            c0 = first + part * count + a // C_OUT
+            return out[t * P : (t + 1) * P, c0 : c0 + w // C_OUT, :].rearrange("p c d -> p (c d)")
+
         def finish(m):
             weight, first, count, is_complex = orders[m]
             width = count * C_OUT
             for t in range(EDGE_TILES):
-                for part in range(2 if is_complex else 1):
-                    stage = result.tile([P, width], F32)
+                for part in range(2):
+                    stage = result.tile([P, width], F32, tag="stage", name="stage%d_%d_%d" % (m, t, part))
                     for a, w in power_of_two_pieces(width, BANK):
-                        if not is_complex:
-                            nc.vector.tensor_tensor(
-                                out=stage[:, a : a + w],
-                                in0=acc[(m, t, part, a)][:, 0:w],
-                                in1=bias[:, a : a + w],
-                                op=mybir.AluOpType.add,
-                            )
-                        else:
-                            nc.scalar.copy(out=stage[:, a : a + w], in_=acc[(m, t, part, a)][:, 0:w])
-                    c0 = first + part * count
-                    stores.append((out[t * P : (t + 1) * P, c0 : c0 + count, :].rearrange("p c d -> p (c d)"), stage))
+                        nc.scalar.copy(out=stage[:, a : a + w], in_=acc[(m, t, part, a)][:, 0:w])
+                    stores.append((rows_of_out(m, t, part, 0, width), stage[:]))
 
-        for i in range(RAW_PASSES):
-            load(i)
-        for s in range(len(passes) + 2):
-            if s < len(passes):
-                regroup(s)
+        def finish_real(m, pieces):
+            start = pieces[0][0]
+            width = pieces[-1][0] + pieces[-1][1] - start
+            for t in range(EDGE_TILES):
+                stage = result.tile([P, width], F32, tag="stage", name="real%d_%d" % (t, start))
+                for a, w in pieces:
+                    nc.vector.tensor_tensor(
+                        out=stage[:, a - start : a - start + w],
+                        in0=acc[(m, t, 0, a)][:, 0:w],
+                        in1=bias[:, a : a + w],
+                        op=mybir.AluOpType.add,
+                    )
+                nc.sync.dma_start(out=rows_of_out(m, t, 0, start, width), in_=stage[:])
+
+        for i in range(1, RAW_PASSES + 1):
+            half = orders[passes[i][0]][0].shape[1] // 2
+            load(i, [(half, 2 * half), (0, half)] if i == 1 else None)
+        last = len(passes) - 1
+        first_block = [(0, BANK)]
+        second_block = power_of_two_pieces(7 * C_OUT, BANK)[1:]
+        for s in range(1, len(passes)):
+            ready = list(stores)
+            stores.clear()
+            n_cols = orders[passes[s][0]][0].shape[1]
+            cut = n_cols // 2 + SCALAR_MORE
+            if s in (8, 9, 13, 14):
+                cut -= SCALAR_LESS
+            if s < last:
+                regroup(s, nc.vector.tensor_copy, cut, n_cols)
+                regroup(s, nc.scalar.copy, 0, cut)
+            else:
+                regroup(s, nc.vector.tensor_copy, LAST_A, BANK)
+                regroup(s, nc.scalar.copy, 0, LAST_A)
+                regroup(s, nc.vector.tensor_copy, LAST_B, n_cols)
+                regroup(s, nc.scalar.copy, BANK, LAST_B)
             if s + RAW_PASSES < len(passes):
-                load(s + RAW_PASSES)
-            if 1 <= s <= len(passes):
-                quantise(s - 1)
+                load(s + RAW_PASSES, None)
+            for target, stage in ready:
+                nc.sync.dma_start(out=target, in_=stage)
             if s >= 2:
+                quantise(s - 1, power_of_two_pieces(orders[passes[s - 1][0]][0].shape[1], 1024))
                 m, g = passes[s - 2]
                 if g == orders[m][2] - 1:
                     finish(m)
-            if 1 <= s <= len(passes):
-                multiply(s - 1)
-            if s + RAW_PASSES >= len(passes) - 1:
-                for target, stage in stores:
-                    nc.sync.dma_start(out=target, in_=stage[:])
-                stores = []
+            multiply(s - 1)
+        quantise(last, first_block)
+        multiply(last, first_block)
+        quantise(last, second_block)
+        multiply(last, second_block)
+        finish_real(2, first_block)
+        finish_real(2, second_block)

@@ -52,12 +52,9 @@ def tile_so2convolution_kernel(tc, edge_feats, edge_embeds, W0, b0, W1, W2, out)
         ctx.enter_context(tc.manual_schedule())
         const = ctx.enter_context(tc.tile_pool(name="const", bufs=1))
         feats = ctx.enter_context(tc.tile_pool(name="feats", bufs=1))
-        xload = ctx.enter_context(tc.tile_pool(name="xload", bufs=3))
-        xwork = ctx.enter_context(tc.tile_pool(name="xwork", bufs=5))
         wload = ctx.enter_context(tc.tile_pool(name="wload", bufs=RAW_PASSES))
         wwork = ctx.enter_context(tc.tile_pool(name="wwork", bufs=3))
-        wquant = ctx.enter_context(tc.tile_pool(name="wquant", bufs=3))
-        result = ctx.enter_context(tc.tile_pool(name="result", bufs=8))
+        wquant = ctx.enter_context(tc.tile_pool(name="wquant", bufs=6))
         psum = ctx.enter_context(tc.psum_pool(name="psum", bufs=8))
 
         identity = const.tile([P, P], F32)
@@ -122,36 +119,41 @@ def tile_so2convolution_kernel(tc, edge_feats, edge_embeds, W0, b0, W1, W2, out)
                 n_coeffs = min(LOAD_COEFFS if loads else LOAD_COEFFS // 2, last - c0)
                 loads.append((c0, n_coeffs))
                 c0 += n_coeffs
-        for c0, n_coeffs in loads:
-            xraw = xload.tile([P, EDGE_TILES * n_coeffs * K_PASS], BF16)
-            nc.sync.dma_start(
-                out=xraw[:].rearrange("p (t x) -> p t x", t=EDGE_TILES),
-                in_=edge_feats[:, c0 : c0 + n_coeffs, :].rearrange("(t p) c k -> p t (c k)", p=P),
-            )
-            xwords = xraw[:].bitcast(F32)
-            for j in range(n_coeffs):
-                c = c0 + j
-                bank = psum.tile([P, BANK], F32, tag="bank")
-                for t in range(EDGE_TILES):
-                    for u in range(2):
-                        w0 = (t * n_coeffs + j) * 2 * P
-                        s = 2 * t + u
-                        nc.tensor.transpose(bank[:, s * P : (s + 1) * P], xwords[:, w0 + u : w0 + 2 * P : 2], identity[:])
-                xg = xwork.tile([P, EDGE_TILES * P * PACK], BF16, align_bytes=64)
-                nc.scalar.copy(
-                    out=xg[:].bitcast(F32).rearrange("p (t e u) -> p t e u", t=EDGE_TILES, u=2),
-                    in_=bank[:].rearrange("p (t u e) -> p t e u", t=EDGE_TILES, u=2),
+        with ExitStack() as features:
+            xload = features.enter_context(tc.tile_pool(name="xload", bufs=3))
+            xwork = features.enter_context(tc.tile_pool(name="xwork", bufs=5))
+            for c0, n_coeffs in loads:
+                xraw = xload.tile([P, EDGE_TILES * n_coeffs * K_PASS], BF16)
+                nc.sync.dma_start(
+                    out=xraw[:].rearrange("p (t x) -> p t x", t=EDGE_TILES),
+                    in_=edge_feats[:, c0 : c0 + n_coeffs, :].rearrange("(t p) c k -> p t (c k)", p=P),
                 )
-                if c in imaginary:
-                    xn = xwork.tile([P, EDGE_TILES * P * PACK], BF16, align_bytes=64)
-                    nc.vector.tensor_scalar_mul(out=xn[:], in0=xg[:], scalar1=-1.0)
-                x_codes[c] = feats.tile([P, EDGE_TILES * P], U32, name="xq%d" % c, align_bytes=64)
-                x_scales[c] = feats.tile([P, EDGE_TILES * P], U8, name="xs%d" % c, align_bytes=64)
-                nc.vector.quantize_mx(out=x_codes[c][:].bitcast(FP8X4), scales=x_scales[c][:], in_=xg[:])
-                if c in imaginary:
-                    neg_codes[c] = feats.tile([P, EDGE_TILES * P], U32, name="nq%d" % c, align_bytes=64)
-                    neg_scales[c] = feats.tile([P, EDGE_TILES * P], U8, name="ns%d" % c, align_bytes=64)
-                    nc.vector.quantize_mx(out=neg_codes[c][:].bitcast(FP8X4), scales=neg_scales[c][:], in_=xn[:])
+                xwords = xraw[:].bitcast(F32)
+                for j in range(n_coeffs):
+                    c = c0 + j
+                    bank = psum.tile([P, BANK], F32, tag="bank")
+                    for t in range(EDGE_TILES):
+                        for u in range(2):
+                            w0 = (t * n_coeffs + j) * 2 * P
+                            s = 2 * t + u
+                            nc.tensor.transpose(bank[:, s * P : (s + 1) * P], xwords[:, w0 + u : w0 + 2 * P : 2], identity[:])
+                    xg = xwork.tile([P, EDGE_TILES * P * PACK], BF16, align_bytes=64)
+                    nc.scalar.copy(
+                        out=xg[:].bitcast(F32).rearrange("p (t e u) -> p t e u", t=EDGE_TILES, u=2),
+                        in_=bank[:].rearrange("p (t u e) -> p t e u", t=EDGE_TILES, u=2),
+                    )
+                    if c in imaginary:
+                        xn = xwork.tile([P, EDGE_TILES * P * PACK], BF16, align_bytes=64)
+                        nc.vector.tensor_scalar_mul(out=xn[:], in0=xg[:], scalar1=-1.0)
+                    x_codes[c] = feats.tile([P, EDGE_TILES * P], U32, name="xq%d" % c, align_bytes=64)
+                    x_scales[c] = feats.tile([P, EDGE_TILES * P], U8, name="xs%d" % c, align_bytes=64)
+                    nc.vector.quantize_mx(out=x_codes[c][:].bitcast(FP8X4), scales=x_scales[c][:], in_=xg[:])
+                    if c in imaginary:
+                        neg_codes[c] = feats.tile([P, EDGE_TILES * P], U32, name="nq%d" % c, align_bytes=64)
+                        neg_scales[c] = feats.tile([P, EDGE_TILES * P], U8, name="ns%d" % c, align_bytes=64)
+                        nc.vector.quantize_mx(out=neg_codes[c][:].bitcast(FP8X4), scales=neg_scales[c][:], in_=xn[:])
+
+        result = ctx.enter_context(tc.tile_pool(name="result", bufs=8))
 
         bias = const.tile([P, 7 * C_OUT], BF16)
         spread = psum.tile([P, 2 * BANK], BF16, tag="bank")

@@ -18,7 +18,7 @@ BANK = 512
 LOAD_COEFFS = 4
 SCALAR_MORE = 16
 SCALAR_LESS = 96
-HEAD_CUT = 640
+HEAD_CUT = 768
 LAST_A = 384
 LAST_B = 768
 RAW_PASSES = 4
@@ -54,7 +54,7 @@ def tile_so2convolution_kernel(tc, edge_feats, edge_embeds, W0, b0, W1, W2, out)
         feats = ctx.enter_context(tc.tile_pool(name="feats", bufs=1))
         wload = ctx.enter_context(tc.tile_pool(name="wload", bufs=RAW_PASSES))
         wwork = ctx.enter_context(tc.tile_pool(name="wwork", bufs=3))
-        wquant = ctx.enter_context(tc.tile_pool(name="wquant", bufs=6))
+        wquant = ctx.enter_context(tc.tile_pool(name="wquant", bufs=4))
         psum = ctx.enter_context(tc.psum_pool(name="psum", bufs=8))
 
         identity = const.tile([P, P], F32)
@@ -102,10 +102,9 @@ def tile_so2convolution_kernel(tc, edge_feats, edge_embeds, W0, b0, W1, W2, out)
                     in_=grouped[i][:, a : a + w, :].rearrange("p w j -> p (w j)"),
                 )
 
-        load(0, [(2 * BANK, 3 * BANK), (0, HEAD_CUT), (HEAD_CUT, 2 * BANK)])
-        regroup(0, nc.vector.tensor_copy, 2 * BANK, 3 * BANK)
+        load(0, [(HEAD_CUT, 3 * BANK), (0, HEAD_CUT)])
         regroup(0, nc.scalar.copy, 0, HEAD_CUT)
-        regroup(0, nc.vector.tensor_copy, HEAD_CUT, 2 * BANK)
+        regroup(0, nc.vector.tensor_copy, HEAD_CUT, 3 * BANK)
         quantise(0, [(2 * BANK, BANK), (0, 2 * BANK)])
 
         x_codes = {}
@@ -222,7 +221,7 @@ def tile_so2convolution_kernel(tc, edge_feats, edge_embeds, W0, b0, W1, W2, out)
 
         for i in range(1, RAW_PASSES + 1):
             half = orders[passes[i][0]][0].shape[1] // 2
-            load(i, [(half, 2 * half), (0, half)] if i == 1 else None)
+            load(i, None)
         last = len(passes) - 1
         first_block = [(0, BANK)]
         second_block = power_of_two_pieces(7 * C_OUT, BANK)[1:]

@@ -16,9 +16,10 @@ C_OUT = 128
 EDGE_TILES = 2
 BANK = 512
 LOAD_COEFFS = 4
-SCALAR_MORE = 16
-SCALAR_LESS = 96
-HEAD_CUT = 768
+SHARE = [832, 640, 384]
+BSHARE = [0, 384, 256]
+BURST = (7, 8, 12, 13)
+HEAD_CUT = 640
 LAST_A = 384
 LAST_B = 768
 RAW_PASSES = 4
@@ -102,7 +103,7 @@ def tile_so2convolution_kernel(tc, edge_feats, edge_embeds, W0, b0, W1, W2, out)
                     in_=grouped[i][:, a : a + w, :].rearrange("p w j -> p (w j)"),
                 )
 
-        load(0, [(HEAD_CUT, 3 * BANK), (0, HEAD_CUT)])
+        load(0, None)
         regroup(0, nc.scalar.copy, 0, HEAD_CUT)
         regroup(0, nc.vector.tensor_copy, HEAD_CUT, 3 * BANK)
         quantise(0, [(2 * BANK, BANK), (0, 2 * BANK)])
@@ -229,9 +230,9 @@ def tile_so2convolution_kernel(tc, edge_feats, edge_embeds, W0, b0, W1, W2, out)
             ready = list(stores)
             stores.clear()
             n_cols = orders[passes[s][0]][0].shape[1]
-            cut = n_cols // 2 + SCALAR_MORE
-            if s in (8, 9, 13, 14):
-                cut -= SCALAR_LESS
+            cut = SHARE[passes[s][0]]
+            if s in BURST:
+                cut = BSHARE[passes[s][0]]
             if s < last:
                 regroup(s, nc.vector.tensor_copy, cut, n_cols)
                 regroup(s, nc.scalar.copy, 0, cut)

from contextlib import ExitStack

import concourse.mybir as mybir
from concourse.masks import make_identity

F32 = mybir.dt.float32
BF16 = mybir.dt.bfloat16
U32 = mybir.dt.uint32
U8 = mybir.dt.uint8
FP8X4 = mybir.dt.float8_e4m3fn_x4

P = 128
PACK = 4
K_PASS = P * PACK
C_OUT = 128
EDGE_TILES = 2
BANK = 512
LOAD_COEFFS = 4
SHARE = [832, 640, 384]
BSHARE = [0, 384, 256]
BURST = (7, 8, 12, 13)
HEAD_CUT = 640
LAST_A = 384
LAST_B = 768
RAW_PASSES = 4

FLOPS = 2 * 256 * (3584 * 896 + 2 * 3072 * 1536 + 2 * 2560 * 1280)


def power_of_two_pieces(width, largest):
    pieces = []
    start = 0
    size = largest
    while start < width:
        while size > width - start:
            size = size // 2
        pieces.append((start, size))
        start += size
    return pieces


def tile_so2convolution_kernel(tc, edge_feats, edge_embeds, W0, b0, W1, W2, out):
    nc = tc.nc
    orders = [(W1, 7, 6, True), (W2, 19, 5, True), (W0, 0, 7, False)]
    passes = []
    imaginary = []
    for m, (weight, first, count, is_complex) in enumerate(orders):
        passes.extend([(m, g) for g in range(count)])
        if is_complex:
            imaginary.extend(range(first + count, first + 2 * count))

    with ExitStack() as ctx:
        ctx.enter_context(tc.manual_schedule())
        const = ctx.enter_context(tc.tile_pool(name="const", bufs=1))
        feats = ctx.enter_context(tc.tile_pool(name="feats", bufs=1))
        wload = ctx.enter_context(tc.tile_pool(name="wload", bufs=RAW_PASSES))
        wwork = ctx.enter_context(tc.tile_pool(name="wwork", bufs=3))
        wquant = ctx.enter_context(tc.tile_pool(name="wquant", bufs=4))
        psum = ctx.enter_context(tc.psum_pool(name="psum", bufs=8))

        identity = const.tile([P, P], F32)
        make_identity(nc, identity[:])

        ones = const.tile([P, P], BF16)
        nc.vector.memset(ones[:], 1.0)
        bias_row = const.tile([P, 2 * BANK], BF16)
        nc.vector.memset(bias_row[:], 0.0)
        nc.scalar.dma_start(out=bias_row[0:1, 0 : 7 * C_OUT], in_=b0.rearrange("(o n) -> o n", o=1))

        raw = {}
        grouped = {}
        w_codes = {}
        w_scales = {}
        acc = {}
        stores = []

        def load(i, cuts):
            m, g = passes[i]
            weight = orders[m][0]
            raw[i] = wload.tile([P, PACK, weight.shape[1]], BF16, name="wraw%d" % i, tag="wraw")
            rows = weight[g * K_PASS : (g + 1) * K_PASS, :].rearrange("(p j) n -> p j n", j=PACK)
            for a, b in cuts or [(0, weight.shape[1])]:
                nc.sync.dma_start(out=raw[i][:, :, a:b], in_=rows[:, :, a:b])

        def regroup(i, engine_copy, a, b):
            if i not in grouped:
                n_cols = orders[passes[i][0]][0].shape[1]
                grouped[i] = wwork.tile([P, n_cols, PACK], BF16, name="wg%d" % i, tag="wg", align_bytes=64)
            engine_copy(
                out=grouped[i][:, a:b, :].rearrange("p (c i) t -> p c t i", i=8),
                in_=raw[i][:, :, a:b].rearrange("p t (c i) -> p c t i", i=8),
            )

        def quantise(i, parts):
            n_cols = orders[passes[i][0]][0].shape[1]
            if i not in w_codes:
                w_codes[i] = wquant.tile([P, n_cols], U32, name="wq%d" % i, tag="wq", align_bytes=64)
                w_scales[i] = wquant.tile([P, n_cols], U8, name="ws%d" % i, tag="ws", align_bytes=64)
            for a, w in parts:
                nc.vector.quantize_mx(
                    out=w_codes[i][:, a : a + w].bitcast(FP8X4),
                    scales=w_scales[i][:, a : a + w],
                    in_=grouped[i][:, a : a + w, :].rearrange("p w j -> p (w j)"),
                )

        load(0, None)
        regroup(0, nc.scalar.copy, 0, HEAD_CUT)
        regroup(0, nc.vector.tensor_copy, HEAD_CUT, 3 * BANK)
        quantise(0, [(2 * BANK, BANK), (0, 2 * BANK)])

        x_codes = {}
        x_scales = {}
        neg_codes = {}
        neg_scales = {}
        loads = []
        for first, last in [(7, 29), (0, 7)]:
            c0 = first
            while c0 < last:
                n_coeffs = min(LOAD_COEFFS if loads else LOAD_COEFFS // 2, last - c0)
                loads.append((c0, n_coeffs))
                c0 += n_coeffs
        with ExitStack() as features:
            xload = features.enter_context(tc.tile_pool(name="xload", bufs=3))
            xwork = features.enter_context(tc.tile_pool(name="xwork", bufs=5))
            for c0, n_coeffs in loads:
                xraw = xload.tile([P, EDGE_TILES * n_coeffs * K_PASS], BF16)
                nc.sync.dma_start(
                    out=xraw[:].rearrange("p (t x) -> p t x", t=EDGE_TILES),
                    in_=edge_feats[:, c0 : c0 + n_coeffs, :].rearrange("(t p) c k -> p t (c k)", p=P),
                )
                xwords = xraw[:].bitcast(F32)
                for j in range(n_coeffs):
                    c = c0 + j
                    bank = psum.tile([P, BANK], F32, tag="bank")
                    for t in range(EDGE_TILES):
                        for u in range(2):
                            w0 = (t * n_coeffs + j) * 2 * P
                            s = 2 * t + u
                            nc.tensor.transpose(bank[:, s * P : (s + 1) * P], xwords[:, w0 + u : w0 + 2 * P : 2], identity[:])
                    xg = xwork.tile([P, EDGE_TILES * P * PACK], BF16, align_bytes=64)
                    nc.scalar.copy(
                        out=xg[:].bitcast(F32).rearrange("p (t e u) -> p t e u", t=EDGE_TILES, u=2),
                        in_=bank[:].rearrange("p (t u e) -> p t e u", t=EDGE_TILES, u=2),
                    )
                    if c in imaginary:
                        xn = xwork.tile([P, EDGE_TILES * P * PACK], BF16, align_bytes=64)
                        nc.vector.tensor_scalar_mul(out=xn[:], in0=xg[:], scalar1=-1.0)
                    x_codes[c] = feats.tile([P, EDGE_TILES * P], U32, name="xq%d" % c, align_bytes=64)
                    x_scales[c] = feats.tile([P, EDGE_TILES * P], U8, name="xs%d" % c, align_bytes=64)
                    nc.vector.quantize_mx(out=x_codes[c][:].bitcast(FP8X4), scales=x_scales[c][:], in_=xg[:])
                    if c in imaginary:
                        neg_codes[c] = feats.tile([P, EDGE_TILES * P], U32, name="nq%d" % c, align_bytes=64)
                        neg_scales[c] = feats.tile([P, EDGE_TILES * P], U8, name="ns%d" % c, align_bytes=64)
                        nc.vector.quantize_mx(out=neg_codes[c][:].bitcast(FP8X4), scales=neg_scales[c][:], in_=xn[:])

        result = ctx.enter_context(tc.tile_pool(name="result", bufs=8))

        bias = const.tile([P, 7 * C_OUT], BF16)
        spread = psum.tile([P, 2 * BANK], BF16, tag="bank")
        for a, b in [(0, BANK), (BANK, 7 * C_OUT)]:
            nc.tensor.matmul(spread[:, a:b], lhsT=ones[:], rhs=bias_row[:, a:b], start=True, stop=True)
        nc.vector.tensor_copy(out=bias[:], in_=spread[:, 0 : 7 * C_OUT])

        def multiply(i, chosen=None):
            m, g = passes[i]
            weight, first, count, is_complex = orders[m]
            width = count * C_OUT
            re = first + g
            im = first + count + g
            for t in range(EDGE_TILES):
                edges = slice(t * P, (t + 1) * P)
                for part in range(2 if is_complex else 1):
                    if not is_complex:
                        terms = [(x_codes[re], x_scales[re], 0)]
                    elif part == 0:
                        terms = [(x_codes[re], x_scales[re], 0), (neg_codes[im], neg_scales[im], width)]
                    else:
                        terms = [(x_codes[im], x_scales[im], 0), (x_codes[re], x_scales[re], width)]
                    for a, w in chosen or power_of_two_pieces(width, BANK):
                        if g == 0:
                            acc[(m, t, part, a)] = psum.tile([P, BANK], F32, tag="bank", name="acc_%d_%d_%d_%d" % (m, t, part, a))
                        for k, (codes, scales, offset) in enumerate(terms):
                            cols = slice(offset + a, offset + a + w)
                            nc.tensor.matmul_mx(
                                out=acc[(m, t, part, a)][:, 0:w],
                                lhsT=codes[:, edges].bitcast(FP8X4),
                                lhsT_scale=scales[:, edges],
                                rhs=w_codes[i][:, cols].bitcast(FP8X4),
                                rhs_scale=w_scales[i][:, cols],
                                start=(g == 0 and k == 0),
                                stop=(g == count - 1 and k == len(terms) - 1),
                            )

        def rows_of_out(m, t, part, a, w):
            weight, first, count, is_complex = orders[m]
            c0 = first + part * count + a // C_OUT
            return out[t * P : (t + 1) * P, c0 : c0 + w // C_OUT, :].rearrange("p c d -> p (c d)")

        def finish(m):
            weight, first, count, is_complex = orders[m]
            width = count * C_OUT
            for t in range(EDGE_TILES):
                for part in range(2):
                    stage = result.tile([P, width], F32, tag="stage", name="stage%d_%d_%d" % (m, t, part))
                    for a, w in power_of_two_pieces(width, BANK):
                        nc.scalar.copy(out=stage[:, a : a + w], in_=acc[(m, t, part, a)][:, 0:w])
                    stores.append((rows_of_out(m, t, part, 0, width), stage[:]))

        def finish_real(m, pieces):
            start = pieces[0][0]
            width = pieces[-1][0] + pieces[-1][1] - start
            for t in range(EDGE_TILES):
                stage = result.tile([P, width], F32, tag="stage", name="real%d_%d" % (t, start))
                for a, w in pieces:
                    nc.vector.tensor_tensor(
                        out=stage[:, a - start : a - start + w],
                        in0=acc[(m, t, 0, a)][:, 0:w],
                        in1=bias[:, a : a + w],
                        op=mybir.AluOpType.add,
                    )
                nc.sync.dma_start(out=rows_of_out(m, t, 0, start, width), in_=stage[:])

        for i in range(1, RAW_PASSES + 1):
            half = orders[passes[i][0]][0].shape[1] // 2
            load(i, None)
        last = len(passes) - 1
        first_block = [(0, BANK)]
        second_block = power_of_two_pieces(7 * C_OUT, BANK)[1:]
        for s in range(1, len(passes)):
            ready = list(stores)
            stores.clear()
            n_cols = orders[passes[s][0]][0].shape[1]
            cut = SHARE[passes[s][0]]
            if s in BURST:
                cut = BSHARE[passes[s][0]]
            if s < last:
                regroup(s, nc.vector.tensor_copy, cut, n_cols)
                regroup(s, nc.scalar.copy, 0, cut)
            else:
                regroup(s, nc.vector.tensor_copy, LAST_A, BANK)
                regroup(s, nc.scalar.copy, 0, LAST_A)
                regroup(s, nc.vector.tensor_copy, LAST_B, n_cols)
                regroup(s, nc.scalar.copy, BANK, LAST_B)
            if s + RAW_PASSES < len(passes):
                load(s + RAW_PASSES, None)
            for target, stage in ready:
                nc.sync.dma_start(out=target, in_=stage)
            if s >= 2:
                quantise(s - 1, power_of_two_pieces(orders[passes[s - 1][0]][0].shape[1], 1024))
                m, g = passes[s - 2]
                if g == orders[m][2] - 1:
                    finish(m)
            multiply(s - 1)
        quantise(last, first_block)
        multiply(last, first_block)
        quantise(last, second_block)
        multiply(last, second_block)
        finish_real(2, first_block)
        finish_real(2, second_block)
